import numpy as np
import ml_dtypes


def mxq(x, axis, fmt="e4m3"):
    dtype, down = {"e4m3": (ml_dtypes.float8_e4m3fn, 7), "e5m2": (ml_dtypes.float8_e5m2, 14)}[fmt]
    v = np.moveaxis(np.asarray(x, np.float32).astype(ml_dtypes.bfloat16).astype(np.float64), axis, -1)
    blocks = v.reshape(v.shape[:-1] + (-1, 32))
    amax = np.abs(blocks).max(-1, keepdims=True)
    byte = np.maximum(np.where(amax > 0, np.frexp(amax)[1] - 1 + 127, 0) - down, 1)
    scale = np.exp2(byte - 127.0)
    codes = (blocks / scale).astype(np.float32).astype(dtype).astype(np.float64)
    return np.moveaxis((codes * scale).reshape(v.shape), -1, axis)


WIDE = False


def mx_kscale(k):
    if not WIDE:
        return np.ones(k)
    levels = np.array([10, -10, 5, -5, 0])
    a = np.random.permutation(np.resize(levels, k // 512 * 4)).reshape(k // 512, 4)
    idx = np.arange(k)
    return np.exp2(a[idx // 512, idx % 128 // 32])


BF16 = ml_dtypes.bfloat16


def bf(x):
    return np.asarray(x, np.float32).astype(BF16)


def f64(x):
    return np.asarray(x).astype(np.float64)


B, N, F, O, E, K = 16, 512, 512, 16, 16, 3


def setup_inputs():
    s = mx_kscale(F)
    return {"x_g": bf(np.random.standard_normal((B, K, N, F)) * s),
            "emb": bf(np.random.standard_normal((B, N, E))),
            "weights_pool": bf(np.random.standard_normal((E, K, F, O)) * 0.5 / np.sqrt(K * F) / s[:, None]),
            "bias_pool": bf(np.random.standard_normal((E, O)) * 0.3)}


def reference(x_g, emb, weights_pool, bias_pool):
    xg, w, g = f64(x_g), f64(weights_pool), f64(emb)
    z = 0.0
    for k in range(K):
        wk = w[:, k].transpose(1, 0, 2).reshape(F, E * O)
        z = z + (mxq(xg[:, k], 2, "e4m3") @ mxq(wk, 0, "e4m3"))
    z = z.reshape(B, N, E, O)
    out = (g[:, :, :, None] * z).sum(2)
    return out + (g[:, :, :, None] * f64(bias_pool)[None, None, :, :]).sum(2)

@@ -1,0 +1,196 @@
+from contextlib import ExitStack
+
+import concourse.mybir as mybir
+from concourse.masks import make_identity
+
+BF16 = mybir.dt.bfloat16
+F32 = mybir.dt.float32
+U32 = mybir.dt.uint32
+U8 = mybir.dt.uint8
+FP8X4 = mybir.dt.float8_e4m3fn_x4
+ADD = mybir.AluOpType.add
+MULT = mybir.AluOpType.mult
+AX = mybir.AxisListType.X
+
+P = 128
+B, KC, N, F, O, E = 16, 3, 512, 512, 16, 16
+NT = N // P
+UNITS = KC * NT
+NB = 6
+
+FLOPS = 2 * B * N * KC * F * E * O + 4 * B * N * E * O
+
+
+def tile_dygcn_pb_t_kernel(tc, x_g, emb, weights_pool, bias_pool, out):
+    nc = tc.nc
+    with ExitStack() as ctx:
+        const = ctx.enter_context(tc.tile_pool(name="const", bufs=1))
+        xpool = ctx.enter_context(tc.tile_pool(name="xpool", bufs=NB))
+        gpool = ctx.enter_context(tc.tile_pool(name="gpool", bufs=3))
+        cpool = ctx.enter_context(tc.tile_pool(name="cpool", bufs=3))
+        ppool = ctx.enter_context(tc.tile_pool(name="ppool", bufs=2))
+        ps_t = ctx.enter_context(tc.psum_pool(name="ps_t", bufs=6))
+        ps_z = ctx.enter_context(tc.psum_pool(name="ps_z", bufs=2))
+        ctx.enter_context(tc.manual_schedule())
+
+        ident_f = const.tile([P, P], F32, name="ident_f")
+        ident_b = const.tile([P, P], BF16, name="ident_b")
+        w_raw = const.tile([P, KC, E, 64], BF16, name="w_raw")
+        w_grp = const.tile([P, KC, 1024], BF16, name="w_grp", align_bytes=64)
+        w_cod = const.tile([P, KC * 256], U32, name="w_cod", align_bytes=64)
+        w_scl = const.tile([P, KC * 256], U8, name="w_scl", align_bytes=64)
+        g_bf = const.tile([P, B * NT * E], BF16, name="g_bf")
+        g_32 = const.tile([P, B * NT, E], F32, name="g_32")
+        g_t = const.tile([P, B * NT * E], BF16, name="g_t")
+        bdiag = const.tile([P, P], BF16, name="bdiag")
+        gb = const.tile([P, B * NT * O], F32, name="gb")
+        o_sb = const.tile([P, B * NT * O], F32, name="o_sb")
+
+        xs_of = {}
+        gr_of = {}
+        cd_of = {}
+        sc_of = {}
+        zp_of = {}
+
+        def load_x(b, split):
+            xs = xpool.tile([P, KC * NT * F], BF16, name="xs")
+            xs_of[b] = xs
+            src = x_g[b].rearrange("k (p t) f -> p k (t f)", t=NT)
+            dst = xs[:].rearrange("p (k c) -> p k c", k=KC)
+            if not split:
+                nc.sync.dma_start(out=dst, in_=src)
+            return src, dst
+
+        def transpose_bank(b, j):
+            xw = xs_of[b][:].bitcast(F32)
+            tp = ps_t.tile([P, 512], F32, name="tp", tag="tp")
+            for s in range(4):
+                c0 = P * (4 * j + s)
+                nc.tensor.transpose(tp[:, P * s : P * s + P], xw[:, c0 : c0 + P], ident_f[:])
+            nc.scalar.copy(
+                out=gr_of[b][:, 512 * j : 512 * j + 512].rearrange("p (a n u) -> p a n u", a=2, u=2),
+                in_=tp[:].rearrange("p (a u n) -> p a n u", a=2, u=2),
+            )
+
+        def new_round(b):
+            gr_of[b] = gpool.tile([P, UNITS * 256], F32, name="gr", align_bytes=64)
+            cd_of[b] = cpool.tile([P, UNITS * P], U32, name="cd", align_bytes=64)
+            sc_of[b] = cpool.tile([P, UNITS * P], U8, name="sc", align_bytes=64)
+
+        def quantise(b, q):
+            nc.vector.quantize_mx(
+                out=cd_of[b][:, 512 * q : 512 * q + 512].bitcast(FP8X4),
+                scales=sc_of[b][:, 512 * q : 512 * q + 512],
+                in_=gr_of[b][:, 1024 * q : 1024 * q + 1024].bitcast(BF16),
+            )
+
+        def mx(b):
+            cd = cd_of[b]
+            sc = sc_of[b]
+            for h in range(2):
+                zp = ps_z.tile([P, 512], F32, name="zp", tag="zp")
+                zp_of[(b, h)] = zp
+                for a in range(2):
+                    t = 2 * h + a
+                    for k in range(KC):
+                        un = NT * k + t
+                        nc.tensor.matmul_mx(
+                            out=zp[:, 256 * a : 256 * a + 256],
+                            lhsT=cd[:, P * un : P * un + P].bitcast(FP8X4),
+                            lhsT_scale=sc[:, P * un : P * un + P],
+                            rhs=w_cod[:, 256 * k : 256 * k + 256].bitcast(FP8X4),
+                            rhs_scale=w_scl[:, 256 * k : 256 * k + 256],
+                            start=(k == 0),
+                            stop=(k == KC - 1),
+                        )
+
+        pr_of = {}
+
+        def weigh(b, h):
+            if h == 0:
+                pr_of[b] = ppool.tile([P, NT * O * E], F32, name="pr")
+            t0 = NT * b + 2 * h
+            nc.vector.tensor_tensor(
+                out=pr_of[b][:, 512 * h : 512 * h + 512].rearrange("p (a o e) -> p a o e", a=2, o=O),
+                in0=zp_of[(b, h)][:].rearrange("p (a o e) -> p a o e", a=2, o=O),
+                in1=g_32[:, t0 : t0 + 2, :].unsqueeze(2).to_broadcast([P, 2, O, E]),
+                op=MULT,
+            )
+
+        def finish(b):
+            rs = ppool.tile([P, NT * O], F32, name="rs")
+            nc.vector.tensor_reduce(
+                out=rs[:], in_=pr_of[b][:].rearrange("p (c e) -> p c e", e=E), axis=AX, op=ADD
+            )
+            cols = slice(NT * O * b, NT * O * (b + 1))
+            nc.vector.tensor_tensor(out=o_sb[:, cols], in0=rs[:], in1=gb[:, cols], op=ADD)
+            nc.sync.dma_start(out=out[b].rearrange("(p t) o -> p (t o)", t=NT), in_=o_sb[:, cols])
+
+        make_identity(nc, ident_f[:])
+        make_identity(nc, ident_b[:])
+        nc.vector.memset(bdiag[:], 0.0)
+
+        wv = weights_pool.rearrange("e k (u p c) o -> k u p e (c o)", u=2, p=P, c=2)
+        src0, dst0 = load_x(0, True)
+        for k in range(KC):
+            for u in range(2):
+                nc.sync.dma_start(out=w_raw[:, k, :, 32 * u : 32 * u + 32], in_=wv[k, u])
+            nc.sync.dma_start(out=dst0[:, k, :], in_=src0[:, k, :])
+        nc.sync.dma_start(
+            out=g_bf[:].rearrange("p (b c) -> p b c", b=B),
+            in_=emb.rearrange("b (p t) e -> p b (t e)", t=NT),
+        )
+        for i in range(8):
+            nc.sync.dma_start(out=bdiag[16 * i : 16 * i + 16, 16 * i : 16 * i + 16], in_=bias_pool)
+        for b in range(1, NB):
+            load_x(b, False)
+
+        new_round(0)
+        for k in range(KC):
+            transpose_bank(0, 2 * k)
+            transpose_bank(0, 2 * k + 1)
+            nc.vector.tensor_copy(
+                out=w_grp[:, k, :].rearrange("p (o e t) -> p o e t", o=O, e=E),
+                in_=w_raw[:, k].rearrange("p e (t o) -> p o e t", t=4),
+            )
+            nc.vector.quantize_mx(
+                out=w_cod[:, 256 * k : 256 * k + 256].bitcast(FP8X4),
+                scales=w_scl[:, 256 * k : 256 * k + 256],
+                in_=w_grp[:, k, :],
+            )
+            quantise(0, k)
+
+        for i in range(1, B + 1):
+            if i < B:
+                if i + NB - 1 < B:
+                    load_x(i + NB - 1, False)
+                new_round(i)
+                for j in range(6):
+                    transpose_bank(i, j)
+            if i == 1:
+                tpb = ps_t.tile([P, 1024], BF16, name="tpb", tag="tp")
+                for c in range(8):
+                    nc.tensor.transpose(tpb[:, P * c : P * c + P], g_bf[:, P * c : P * c + P], ident_b[:])
+                nc.scalar.copy(out=g_t[:], in_=tpb[:])
+                nc.vector.tensor_copy(out=g_32[:].rearrange("p t e -> p (t e)"), in_=g_bf[:])
+                for half in range(2):
+                    gp = ps_t.tile([P, 512], F32, name="gp", tag="tp")
+                    for c4 in range(4):
+                        c = 4 * half + c4
+                        nc.tensor.matmul(
+                            gp[:, P * c4 : P * c4 + P],
+                            lhsT=g_t[:, P * c : P * c + P],
+                            rhs=bdiag[:],
+                            start=True,
+                            stop=True,
+                        )
+                    nc.scalar.copy(out=gb[:, 512 * half : 512 * half + 512], in_=gp[:])
+            mx(i - 1)
+            if i < B:
+                quantise(i, 0)
+                quantise(i, 1)
+            weigh(i - 1, 0)
+            if i < B:
+                quantise(i, 2)
+            weigh(i - 1, 1)
+            finish(i - 1)

@@ -17,6 +17,8 @@ B, KC, N, F, O, E = 16, 3, 512, 512, 16, 16
 NT = N // P
 UNITS = KC * NT
 NB = 6
+R = 2 * B
+LAG = 2
 
 FLOPS = 2 * B * N * KC * F * E * O + 4 * B * N * E * O
 
@@ -51,6 +53,7 @@ def tile_dygcn_pb_t_kernel(tc, x_g, emb, weights_pool, bias_pool, out):
         cd_of = {}
         sc_of = {}
         zp_of = {}
+        pr_of = {}
 
         def load_x(b, split):
             xs = xpool.tile([P, KC * NT * F], BF16, name="xs")
@@ -61,50 +64,49 @@ def tile_dygcn_pb_t_kernel(tc, x_g, emb, weights_pool, bias_pool, out):
                 nc.sync.dma_start(out=dst, in_=src)
             return src, dst
 
-        def transpose_bank(b, j):
-            xw = xs_of[b][:].bitcast(F32)
-            tp = ps_t.tile([P, 512], F32, name="tp", tag="tp")
-            for s in range(4):
-                c0 = P * (4 * j + s)
-                nc.tensor.transpose(tp[:, P * s : P * s + P], xw[:, c0 : c0 + P], ident_f[:])
-            nc.scalar.copy(
-                out=gr_of[b][:, 512 * j : 512 * j + 512].rearrange("p (a n u) -> p a n u", a=2, u=2),
-                in_=tp[:].rearrange("p (a u n) -> p a n u", a=2, u=2),
-            )
-
-        def new_round(b):
+        def new_batch(b):
             gr_of[b] = gpool.tile([P, UNITS * 256], F32, name="gr", align_bytes=64)
             cd_of[b] = cpool.tile([P, UNITS * P], U32, name="cd", align_bytes=64)
             sc_of[b] = cpool.tile([P, UNITS * P], U8, name="sc", align_bytes=64)
 
-        def quantise(b, q):
-            nc.vector.quantize_mx(
-                out=cd_of[b][:, 512 * q : 512 * q + 512].bitcast(FP8X4),
-                scales=sc_of[b][:, 512 * q : 512 * q + 512],
-                in_=gr_of[b][:, 1024 * q : 1024 * q + 1024].bitcast(BF16),
+        def transpose_bank(b, h, k):
+            xw = xs_of[b][:].bitcast(F32)
+            tp = ps_t.tile([P, 512], F32, name="tp", tag="tp")
+            for s in range(4):
+                c0 = P * (8 * k + 4 * h + s)
+                nc.tensor.transpose(tp[:, P * s : P * s + P], xw[:, c0 : c0 + P], ident_f[:])
+            g0 = 512 * (3 * h + k)
+            nc.scalar.copy(
+                out=gr_of[b][:, g0 : g0 + 512].rearrange("p (a n u) -> p a n u", a=2, u=2),
+                in_=tp[:].rearrange("p (a u n) -> p a n u", a=2, u=2),
             )
 
-        def mx(b):
+        def quantise(b, h, part):
+            c0 = 768 * h + 512 * part
+            cw = 512 if part == 0 else 256
+            nc.vector.quantize_mx(
+                out=cd_of[b][:, c0 : c0 + cw].bitcast(FP8X4),
+                scales=sc_of[b][:, c0 : c0 + cw],
+                in_=gr_of[b][:, 2 * c0 : 2 * (c0 + cw)].bitcast(BF16),
+            )
+
+        def mx(b, h):
             cd = cd_of[b]
             sc = sc_of[b]
-            for h in range(2):
-                zp = ps_z.tile([P, 512], F32, name="zp", tag="zp")
-                zp_of[(b, h)] = zp
-                for a in range(2):
-                    t = 2 * h + a
-                    for k in range(KC):
-                        un = NT * k + t
-                        nc.tensor.matmul_mx(
-                            out=zp[:, 256 * a : 256 * a + 256],
-                            lhsT=cd[:, P * un : P * un + P].bitcast(FP8X4),
-                            lhsT_scale=sc[:, P * un : P * un + P],
-                            rhs=w_cod[:, 256 * k : 256 * k + 256].bitcast(FP8X4),
-                            rhs_scale=w_scl[:, 256 * k : 256 * k + 256],
-                            start=(k == 0),
-                            stop=(k == KC - 1),
-                        )
-
-        pr_of = {}
+            zp = ps_z.tile([P, 512], F32, name="zp", tag="zp")
+            zp_of[(b, h)] = zp
+            for a in range(2):
+                for k in range(KC):
+                    c0 = P * (6 * h + 2 * k + a)
+                    nc.tensor.matmul_mx(
+                        out=zp[:, 256 * a : 256 * a + 256],
+                        lhsT=cd[:, c0 : c0 + P].bitcast(FP8X4),
+                        lhsT_scale=sc[:, c0 : c0 + P],
+                        rhs=w_cod[:, 256 * k : 256 * k + 256].bitcast(FP8X4),
+                        rhs_scale=w_scl[:, 256 * k : 256 * k + 256],
+                        start=(k == 0),
+                        stop=(k == KC - 1),
+                    )
 
         def weigh(b, h):
             if h == 0:
@@ -126,6 +128,25 @@ def tile_dygcn_pb_t_kernel(tc, x_g, emb, weights_pool, bias_pool, out):
             nc.vector.tensor_tensor(out=o_sb[:, cols], in0=rs[:], in1=gb[:, cols], op=ADD)
             nc.sync.dma_start(out=out[b].rearrange("(p t) o -> p (t o)", t=NT), in_=o_sb[:, cols])
 
+        def bias_product():
+            tpb = ps_t.tile([P, 1024], BF16, name="tpb", tag="tp")
+            for c in range(8):
+                nc.tensor.transpose(tpb[:, P * c : P * c + P], g_bf[:, P * c : P * c + P], ident_b[:])
+            nc.scalar.copy(out=g_t[:], in_=tpb[:])
+            nc.vector.tensor_copy(out=g_32[:].rearrange("p t e -> p (t e)"), in_=g_bf[:])
+            for half in range(2):
+                gp = ps_t.tile([P, 512], F32, name="gp", tag="tp")
+                for c4 in range(4):
+                    c = 4 * half + c4
+                    nc.tensor.matmul(
+                        gp[:, P * c4 : P * c4 + P],
+                        lhsT=g_t[:, P * c : P * c + P],
+                        rhs=bdiag[:],
+                        start=True,
+                        stop=True,
+                    )
+                nc.scalar.copy(out=gb[:, 512 * half : 512 * half + 512], in_=gp[:])
+
         make_identity(nc, ident_f[:])
         make_identity(nc, ident_b[:])
         nc.vector.memset(bdiag[:], 0.0)
@@ -145,10 +166,10 @@ def tile_dygcn_pb_t_kernel(tc, x_g, emb, weights_pool, bias_pool, out):
         for b in range(1, NB):
             load_x(b, False)
 
-        new_round(0)
+        new_batch(0)
         for k in range(KC):
-            transpose_bank(0, 2 * k)
-            transpose_bank(0, 2 * k + 1)
+            transpose_bank(0, 0, k)
+            transpose_bank(0, 1, k)
             nc.vector.tensor_copy(
                 out=w_grp[:, k, :].rearrange("p (o e t) -> p o e t", o=O, e=E),
                 in_=w_raw[:, k].rearrange("p e (t o) -> p o e t", t=4),
@@ -158,39 +179,29 @@ def tile_dygcn_pb_t_kernel(tc, x_g, emb, weights_pool, bias_pool, out):
                 scales=w_scl[:, 256 * k : 256 * k + 256],
                 in_=w_grp[:, k, :],
             )
-            quantise(0, k)
+            if k == 1:
+                quantise(0, 0, 0)
+                quantise(0, 1, 0)
+            if k == 2:
+                quantise(0, 0, 1)
+                quantise(0, 1, 1)
 
-        for i in range(1, B + 1):
-            if i < B:
-                if i + NB - 1 < B:
-                    load_x(i + NB - 1, False)
-                new_round(i)
-                for j in range(6):
-                    transpose_bank(i, j)
-            if i == 1:
-                tpb = ps_t.tile([P, 1024], BF16, name="tpb", tag="tp")
-                for c in range(8):
-                    nc.tensor.transpose(tpb[:, P * c : P * c + P], g_bf[:, P * c : P * c + P], ident_b[:])
-                nc.scalar.copy(out=g_t[:], in_=tpb[:])
-                nc.vector.tensor_copy(out=g_32[:].rearrange("p t e -> p (t e)"), in_=g_bf[:])
-                for half in range(2):
-                    gp = ps_t.tile([P, 512], F32, name="gp", tag="tp")
-                    for c4 in range(4):
-                        c = 4 * half + c4
-                        nc.tensor.matmul(
-                            gp[:, P * c4 : P * c4 + P],
-                            lhsT=g_t[:, P * c : P * c + P],
-                            rhs=bdiag[:],
-                            start=True,
-                            stop=True,
-                        )
-                    nc.scalar.copy(out=gb[:, 512 * half : 512 * half + 512], in_=gp[:])
-            mx(i - 1)
-            if i < B:
-                quantise(i, 0)
-                quantise(i, 1)
-            weigh(i - 1, 0)
-            if i < B:
-                quantise(i, 2)
-            weigh(i - 1, 1)
-            finish(i - 1)
+        for r in range(2, R + LAG):
+            if r < R:
+                b, h = divmod(r, 2)
+                if h == 0:
+                    if b + NB - 1 < B:
+                        load_x(b + NB - 1, False)
+                    new_batch(b)
+                for k in range(KC):
+                    transpose_bank(b, h, k)
+            if r == 2:
+                bias_product()
+            bm, hm = divmod(r - LAG, 2)
+            mx(bm, hm)
+            if r < R:
+                quantise(b, h, 0)
+                quantise(b, h, 1)
+            weigh(bm, hm)
+            if hm == 1:
+                finish(bm)

@@ -17,8 +17,8 @@ B, KC, N, F, O, E = 16, 3, 512, 512, 16, 16
 NT = N // P
 UNITS = KC * NT
 NB = 6
-R = 2 * B
-LAG = 2
+BO = NT * O
+GP_LAST = B - 3
 
 FLOPS = 2 * B * N * KC * F * E * O + 4 * B * N * E * O
 
@@ -30,7 +30,7 @@ def tile_dygcn_pb_t_kernel(tc, x_g, emb, weights_pool, bias_pool, out):
         xpool = ctx.enter_context(tc.tile_pool(name="xpool", bufs=NB))
         gpool = ctx.enter_context(tc.tile_pool(name="gpool", bufs=3))
         cpool = ctx.enter_context(tc.tile_pool(name="cpool", bufs=3))
-        ppool = ctx.enter_context(tc.tile_pool(name="ppool", bufs=2))
+        ppool = ctx.enter_context(tc.tile_pool(name="ppool", bufs=3))
         ps_t = ctx.enter_context(tc.psum_pool(name="ps_t", bufs=6))
         ps_z = ctx.enter_context(tc.psum_pool(name="ps_z", bufs=2))
         ctx.enter_context(tc.manual_schedule())
@@ -45,8 +45,8 @@ def tile_dygcn_pb_t_kernel(tc, x_g, emb, weights_pool, bias_pool, out):
         g_32 = const.tile([P, B * NT, E], F32, name="g_32")
         g_t = const.tile([P, B * NT * E], BF16, name="g_t")
         bdiag = const.tile([P, P], BF16, name="bdiag")
-        gb = const.tile([P, B * NT * O], F32, name="gb")
-        o_sb = const.tile([P, B * NT * O], F32, name="o_sb")
+        gb = const.tile([P, B * BO], F32, name="gb")
+        o_sb = const.tile([P, B * BO], F32, name="o_sb")
 
         xs_of = {}
         gr_of = {}
@@ -54,6 +54,8 @@ def tile_dygcn_pb_t_kernel(tc, x_g, emb, weights_pool, bias_pool, out):
         sc_of = {}
         zp_of = {}
         pr_of = {}
+        q1_of = {}
+        q2_of = {}
 
         def load_x(b, split):
             xs = xpool.tile([P, KC * NT * F], BF16, name="xs")
@@ -69,44 +71,42 @@ def tile_dygcn_pb_t_kernel(tc, x_g, emb, weights_pool, bias_pool, out):
             cd_of[b] = cpool.tile([P, UNITS * P], U32, name="cd", align_bytes=64)
             sc_of[b] = cpool.tile([P, UNITS * P], U8, name="sc", align_bytes=64)
 
-        def transpose_bank(b, h, k):
+        def transpose_bank(b, j):
             xw = xs_of[b][:].bitcast(F32)
             tp = ps_t.tile([P, 512], F32, name="tp", tag="tp")
             for s in range(4):
-                c0 = P * (8 * k + 4 * h + s)
+                c0 = P * (4 * j + s)
                 nc.tensor.transpose(tp[:, P * s : P * s + P], xw[:, c0 : c0 + P], ident_f[:])
-            g0 = 512 * (3 * h + k)
             nc.scalar.copy(
-                out=gr_of[b][:, g0 : g0 + 512].rearrange("p (a n u) -> p a n u", a=2, u=2),
+                out=gr_of[b][:, 512 * j : 512 * j + 512].rearrange("p (a n u) -> p a n u", a=2, u=2),
                 in_=tp[:].rearrange("p (a u n) -> p a n u", a=2, u=2),
             )
 
-        def quantise(b, h, part):
-            c0 = 768 * h + 512 * part
-            cw = 512 if part == 0 else 256
+        def quantise(b, c0, cw):
             nc.vector.quantize_mx(
                 out=cd_of[b][:, c0 : c0 + cw].bitcast(FP8X4),
                 scales=sc_of[b][:, c0 : c0 + cw],
                 in_=gr_of[b][:, 2 * c0 : 2 * (c0 + cw)].bitcast(BF16),
             )
 
-        def mx(b, h):
+        def mx(b):
             cd = cd_of[b]
             sc = sc_of[b]
-            zp = ps_z.tile([P, 512], F32, name="zp", tag="zp")
-            zp_of[(b, h)] = zp
-            for a in range(2):
-                for k in range(KC):
-                    c0 = P * (6 * h + 2 * k + a)
-                    nc.tensor.matmul_mx(
-                        out=zp[:, 256 * a : 256 * a + 256],
-                        lhsT=cd[:, c0 : c0 + P].bitcast(FP8X4),
-                        lhsT_scale=sc[:, c0 : c0 + P],
-                        rhs=w_cod[:, 256 * k : 256 * k + 256].bitcast(FP8X4),
-                        rhs_scale=w_scl[:, 256 * k : 256 * k + 256],
-                        start=(k == 0),
-                        stop=(k == KC - 1),
-                    )
+            for h in range(2):
+                zp = ps_z.tile([P, 512], F32, name="zp", tag="zp")
+                zp_of[(b, h)] = zp
+                for a in range(2):
+                    for k in range(KC):
+                        c0 = P * (NT * k + 2 * h + a)
+                        nc.tensor.matmul_mx(
+                            out=zp[:, 256 * a : 256 * a + 256],
+                            lhsT=cd[:, c0 : c0 + P].bitcast(FP8X4),
+                            lhsT_scale=sc[:, c0 : c0 + P],
+                            rhs=w_cod[:, 256 * k : 256 * k + 256].bitcast(FP8X4),
+                            rhs_scale=w_scl[:, 256 * k : 256 * k + 256],
+                            start=(k == 0),
+                            stop=(k == KC - 1),
+                        )
 
         def weigh(b, h):
             if h == 0:
@@ -119,14 +119,40 @@ def tile_dygcn_pb_t_kernel(tc, x_g, emb, weights_pool, bias_pool, out):
                 op=MULT,
             )
 
-        def finish(b):
-            rs = ppool.tile([P, NT * O], F32, name="rs")
-            nc.vector.tensor_reduce(
-                out=rs[:], in_=pr_of[b][:].rearrange("p (c e) -> p c e", e=E), axis=AX, op=ADD
+        def fold_16_to_8(b, h):
+            if h == 0:
+                q1_of[b] = ppool.tile([P, BO * 8], F32, name="q1")
+            pv = pr_of[b][:, 512 * h : 512 * h + 512].rearrange("p (c e) -> p c e", e=E)
+            nc.gpsimd.tensor_tensor(
+                out=q1_of[b][:, 256 * h : 256 * h + 256].rearrange("p (c e) -> p c e", e=8),
+                in0=pv[:, :, 0:8],
+                in1=pv[:, :, 8:16],
+                op=ADD,
             )
-            cols = slice(NT * O * b, NT * O * (b + 1))
-            nc.vector.tensor_tensor(out=o_sb[:, cols], in0=rs[:], in1=gb[:, cols], op=ADD)
-            nc.sync.dma_start(out=out[b].rearrange("(p t) o -> p (t o)", t=NT), in_=o_sb[:, cols])
+
+        def fold_8_to_4(b):
+            if b % 2 == 0:
+                q2_of[b // 2] = ppool.tile([P, 2 * BO * 4], F32, name="q2")
+            qv = q1_of[b][:].rearrange("p (c e) -> p c e", e=8)
+            c0 = 256 * (b % 2)
+            nc.gpsimd.tensor_tensor(
+                out=q2_of[b // 2][:, c0 : c0 + 256].rearrange("p (c e) -> p c e", e=4),
+                in0=qv[:, :, 0:4],
+                in1=qv[:, :, 4:8],
+                op=ADD,
+            )
+
+        def finish(b0, nb, terms, width):
+            rs = ppool.tile([P, 2 * BO], F32, name="rs")
+            nc.vector.tensor_reduce(
+                out=rs[:, 0 : nb * BO], in_=terms.rearrange("p (c e) -> p c e", e=width), axis=AX, op=ADD
+            )
+            cols = slice(BO * b0, BO * (b0 + nb))
+            nc.vector.tensor_tensor(out=o_sb[:, cols], in0=rs[:, 0 : nb * BO], in1=gb[:, cols], op=ADD)
+            nc.sync.dma_start(
+                out=out[b0 : b0 + nb].rearrange("b (p t) o -> p b (t o)", t=NT),
+                in_=o_sb[:, cols].rearrange("p (b c) -> p b c", b=nb),
+            )
 
         def bias_product():
             tpb = ps_t.tile([P, 1024], BF16, name="tpb", tag="tp")
@@ -168,8 +194,8 @@ def tile_dygcn_pb_t_kernel(tc, x_g, emb, weights_pool, bias_pool, out):
 
         new_batch(0)
         for k in range(KC):
-            transpose_bank(0, 0, k)
-            transpose_bank(0, 1, k)
+            transpose_bank(0, 2 * k)
+            transpose_bank(0, 2 * k + 1)
             nc.vector.tensor_copy(
                 out=w_grp[:, k, :].rearrange("p (o e t) -> p o e t", o=O, e=E),
                 in_=w_raw[:, k].rearrange("p e (t o) -> p o e t", t=4),
@@ -179,29 +205,31 @@ def tile_dygcn_pb_t_kernel(tc, x_g, emb, weights_pool, bias_pool, out):
                 scales=w_scl[:, 256 * k : 256 * k + 256],
                 in_=w_grp[:, k, :],
             )
-            if k == 1:
-                quantise(0, 0, 0)
-                quantise(0, 1, 0)
-            if k == 2:
-                quantise(0, 0, 1)
-                quantise(0, 1, 1)
+            quantise(0, 512 * k, 512)
 
-        for r in range(2, R + LAG):
-            if r < R:
-                b, h = divmod(r, 2)
-                if h == 0:
-                    if b + NB - 1 < B:
-                        load_x(b + NB - 1, False)
-                    new_batch(b)
-                for k in range(KC):
-                    transpose_bank(b, h, k)
-            if r == 2:
+        for i in range(1, B + 1):
+            if i < B:
+                if i + NB - 1 < B:
+                    load_x(i + NB - 1, False)
+                new_batch(i)
+                for j in range(6):
+                    transpose_bank(i, j)
+            if i == 1:
                 bias_product()
-            bm, hm = divmod(r - LAG, 2)
-            mx(bm, hm)
-            if r < R:
-                quantise(b, h, 0)
-                quantise(b, h, 1)
-            weigh(bm, hm)
-            if hm == 1:
-                finish(bm)
+            mx(i - 1)
+            if i < B:
+                quantise(i, 0, 1024)
+                quantise(i, 1024, 512)
+            if i == B:
+                finish(B - 2, 1, pr_of[B - 2][:], E)
+            if 0 <= i - 2 <= GP_LAST:
+                fold_8_to_4(i - 2)
+            weigh(i - 1, 0)
+            if i - 1 <= GP_LAST:
+                fold_16_to_8(i - 1, 0)
+            weigh(i - 1, 1)
+            if i - 1 <= GP_LAST:
+                fold_16_to_8(i - 1, 1)
+            if i >= 3 and i % 2 == 1:
+                finish(i - 3, 2, q2_of[(i - 3) // 2][:], 4)
+        finish(B - 1, 1, pr_of[B - 1][:], E)

@@ -89,24 +89,23 @@ def tile_dygcn_pb_t_kernel(tc, x_g, emb, weights_pool, bias_pool, out):
                 in_=gr_of[b][:, 2 * c0 : 2 * (c0 + cw)].bitcast(BF16),
             )
 
-        def mx(b):
+        def mx(b, h):
             cd = cd_of[b]
             sc = sc_of[b]
-            for h in range(2):
-                zp = ps_z.tile([P, 512], F32, name="zp", tag="zp")
-                zp_of[(b, h)] = zp
-                for a in range(2):
-                    for k in range(KC):
-                        c0 = P * (NT * k + 2 * h + a)
-                        nc.tensor.matmul_mx(
-                            out=zp[:, 256 * a : 256 * a + 256],
-                            lhsT=cd[:, c0 : c0 + P].bitcast(FP8X4),
-                            lhsT_scale=sc[:, c0 : c0 + P],
-                            rhs=w_cod[:, 256 * k : 256 * k + 256].bitcast(FP8X4),
-                            rhs_scale=w_scl[:, 256 * k : 256 * k + 256],
-                            start=(k == 0),
-                            stop=(k == KC - 1),
-                        )
+            zp = ps_z.tile([P, 512], F32, name="zp", tag="zp")
+            zp_of[(b, h)] = zp
+            for a in range(2):
+                for k in range(KC):
+                    c0 = P * (NT * k + 2 * h + a)
+                    nc.tensor.matmul_mx(
+                        out=zp[:, 256 * a : 256 * a + 256],
+                        lhsT=cd[:, c0 : c0 + P].bitcast(FP8X4),
+                        lhsT_scale=sc[:, c0 : c0 + P],
+                        rhs=w_cod[:, 256 * k : 256 * k + 256].bitcast(FP8X4),
+                        rhs_scale=w_scl[:, 256 * k : 256 * k + 256],
+                        start=(k == 0),
+                        stop=(k == KC - 1),
+                    )
 
         def weigh(b, h):
             if h == 0:
@@ -176,6 +175,8 @@ def tile_dygcn_pb_t_kernel(tc, x_g, emb, weights_pool, bias_pool, out):
         make_identity(nc, ident_f[:])
         make_identity(nc, ident_b[:])
         nc.vector.memset(bdiag[:], 0.0)
+        for i in range(8):
+            nc.gpsimd.dma_start(out=bdiag[16 * i : 16 * i + 16, 16 * i : 16 * i + 16], in_=bias_pool)
 
         wv = weights_pool.rearrange("e k (u p c) o -> k u p e (c o)", u=2, p=P, c=2)
         src0, dst0 = load_x(0, True)
@@ -187,8 +188,6 @@ def tile_dygcn_pb_t_kernel(tc, x_g, emb, weights_pool, bias_pool, out):
             out=g_bf[:].rearrange("p (b c) -> p b c", b=B),
             in_=emb.rearrange("b (p t) e -> p b (t e)", t=NT),
         )
-        for i in range(8):
-            nc.sync.dma_start(out=bdiag[16 * i : 16 * i + 16, 16 * i : 16 * i + 16], in_=bias_pool)
         for b in range(1, NB):
             load_x(b, False)
 
@@ -207,29 +206,33 @@ def tile_dygcn_pb_t_kernel(tc, x_g, emb, weights_pool, bias_pool, out):
             )
             quantise(0, 512 * k, 512)
 
-        for i in range(1, B + 1):
+        bias_product()
+
+        for i in range(1, B + 2):
             if i < B:
                 if i + NB - 1 < B:
                     load_x(i + NB - 1, False)
                 new_batch(i)
-                for j in range(6):
-                    transpose_bank(i, j)
-            if i == 1:
-                bias_product()
-            mx(i - 1)
-            if i < B:
-                quantise(i, 0, 1024)
-                quantise(i, 1024, 512)
-            if i == B:
+            for h in range(2):
+                if i < B:
+                    for k in range(KC):
+                        transpose_bank(i, 2 * k + h)
+                if i >= 2:
+                    mx(i - 2, h)
+            if 2 <= i <= B:
+                quantise(i - 1, 0, 1024)
+                quantise(i - 1, 1024, 512)
+            if i == B + 1:
                 finish(B - 2, 1, pr_of[B - 2][:], E)
-            if 0 <= i - 2 <= GP_LAST:
-                fold_8_to_4(i - 2)
-            weigh(i - 1, 0)
-            if i - 1 <= GP_LAST:
-                fold_16_to_8(i - 1, 0)
-            weigh(i - 1, 1)
-            if i - 1 <= GP_LAST:
-                fold_16_to_8(i - 1, 1)
-            if i >= 3 and i % 2 == 1:
-                finish(i - 3, 2, q2_of[(i - 3) // 2][:], 4)
+            if 0 <= i - 3 <= GP_LAST:
+                fold_8_to_4(i - 3)
+            if i >= 2:
+                weigh(i - 2, 0)
+                if i - 2 <= GP_LAST:
+                    fold_16_to_8(i - 2, 0)
+                weigh(i - 2, 1)
+                if i - 2 <= GP_LAST:
+                    fold_16_to_8(i - 2, 1)
+            if i >= 4 and i % 2 == 0:
+                finish(i - 4, 2, q2_of[(i - 4) // 2][:], 4)
         finish(B - 1, 1, pr_of[B - 1][:], E)

@@ -30,7 +30,7 @@ def tile_dygcn_pb_t_kernel(tc, x_g, emb, weights_pool, bias_pool, out):
         xpool = ctx.enter_context(tc.tile_pool(name="xpool", bufs=NB))
         gpool = ctx.enter_context(tc.tile_pool(name="gpool", bufs=3))
         cpool = ctx.enter_context(tc.tile_pool(name="cpool", bufs=3))
-        ppool = ctx.enter_context(tc.tile_pool(name="ppool", bufs=3))
+        ppool = ctx.enter_context(tc.tile_pool(name="ppool", bufs=4))
         ps_t = ctx.enter_context(tc.psum_pool(name="ps_t", bufs=6))
         ps_z = ctx.enter_context(tc.psum_pool(name="ps_z", bufs=2))
         ctx.enter_context(tc.manual_schedule())
@@ -55,7 +55,6 @@ def tile_dygcn_pb_t_kernel(tc, x_g, emb, weights_pool, bias_pool, out):
         zp_of = {}
         pr_of = {}
         q1_of = {}
-        q2_of = {}
 
         def load_x(b, split):
             xs = xpool.tile([P, KC * NT * F], BF16, name="xs")
@@ -119,25 +118,14 @@ def tile_dygcn_pb_t_kernel(tc, x_g, emb, weights_pool, bias_pool, out):
             )
 
         def fold_16_to_8(b, h):
-            if h == 0:
-                q1_of[b] = ppool.tile([P, BO * 8], F32, name="q1")
+            if h == 0 and b % 2 == 0:
+                q1_of[b // 2] = ppool.tile([P, 2 * BO * 8], F32, name="q1")
             pv = pr_of[b][:, 512 * h : 512 * h + 512].rearrange("p (c e) -> p c e", e=E)
+            c0 = 512 * (b % 2) + 256 * h
             nc.gpsimd.tensor_tensor(
-                out=q1_of[b][:, 256 * h : 256 * h + 256].rearrange("p (c e) -> p c e", e=8),
+                out=q1_of[b // 2][:, c0 : c0 + 256].rearrange("p (c e) -> p c e", e=8),
                 in0=pv[:, :, 0:8],
                 in1=pv[:, :, 8:16],
-                op=ADD,
-            )
-
-        def fold_8_to_4(b):
-            if b % 2 == 0:
-                q2_of[b // 2] = ppool.tile([P, 2 * BO * 4], F32, name="q2")
-            qv = q1_of[b][:].rearrange("p (c e) -> p c e", e=8)
-            c0 = 256 * (b % 2)
-            nc.gpsimd.tensor_tensor(
-                out=q2_of[b // 2][:, c0 : c0 + 256].rearrange("p (c e) -> p c e", e=4),
-                in0=qv[:, :, 0:4],
-                in1=qv[:, :, 4:8],
                 op=ADD,
             )
 
@@ -213,19 +201,16 @@ def tile_dygcn_pb_t_kernel(tc, x_g, emb, weights_pool, bias_pool, out):
                 if i + NB - 1 < B:
                     load_x(i + NB - 1, False)
                 new_batch(i)
-            for h in range(2):
-                if i < B:
-                    for k in range(KC):
-                        transpose_bank(i, 2 * k + h)
-                if i >= 2:
-                    mx(i - 2, h)
+                for j in range(6):
+                    transpose_bank(i, j)
+            if i >= 2:
+                mx(i - 2, 0)
+                mx(i - 2, 1)
             if 2 <= i <= B:
                 quantise(i - 1, 0, 1024)
                 quantise(i - 1, 1024, 512)
             if i == B + 1:
                 finish(B - 2, 1, pr_of[B - 2][:], E)
-            if 0 <= i - 3 <= GP_LAST:
-                fold_8_to_4(i - 3)
             if i >= 2:
                 weigh(i - 2, 0)
                 if i - 2 <= GP_LAST:
@@ -234,5 +219,5 @@ def tile_dygcn_pb_t_kernel(tc, x_g, emb, weights_pool, bias_pool, out):
                 if i - 2 <= GP_LAST:
                     fold_16_to_8(i - 2, 1)
             if i >= 4 and i % 2 == 0:
-                finish(i - 4, 2, q2_of[(i - 4) // 2][:], 4)
+                finish(i - 4, 2, q1_of[(i - 4) // 2][:], 8)
         finish(B - 1, 1, pr_of[B - 1][:], E)

@@ -37,8 +37,10 @@ def tile_dygcn_pb_t_kernel(tc, x_g, emb, weights_pool, bias_pool, out):
 
         ident_f = const.tile([P, P], F32, name="ident_f")
         ident_b = const.tile([P, P], BF16, name="ident_b")
-        w_raw = const.tile([P, KC, E, 64], BF16, name="w_raw")
-        w_grp = const.tile([P, KC, 1024], BF16, name="w_grp", align_bytes=64)
+        perm_f = const.tile([P, P], F32, name="perm_f")
+        w_nat = const.tile([P, 256 * O], BF16, name="w_nat")
+        w_prm = const.tile([P, O, 256], BF16, name="w_prm")
+        w_grp = const.tile([P, KC * 512], F32, name="w_grp", align_bytes=64)
         w_cod = const.tile([P, KC * 256], U32, name="w_cod", align_bytes=64)
         w_scl = const.tile([P, KC * 256], U8, name="w_scl", align_bytes=64)
         g_bf = const.tile([P, B * NT * E], BF16, name="g_bf")
@@ -163,14 +165,18 @@ def tile_dygcn_pb_t_kernel(tc, x_g, emb, weights_pool, bias_pool, out):
         make_identity(nc, ident_f[:])
         make_identity(nc, ident_b[:])
         nc.vector.memset(bdiag[:], 0.0)
+        nc.vector.memset(w_nat[96:128, :], 0.0)
         for i in range(8):
             nc.gpsimd.dma_start(out=bdiag[16 * i : 16 * i + 16, 16 * i : 16 * i + 16], in_=bias_pool)
+        nc.vector.tensor_copy(
+            out=perm_f[:, 0:96].rearrange("p (k e u) -> p k e u", k=KC, e=E),
+            in_=ident_f[:, 0:96].rearrange("p (e k u) -> p k e u", e=E, k=KC),
+        )
+        nc.vector.tensor_copy(out=perm_f[:, 96:128], in_=ident_f[:, 96:128])
 
-        wv = weights_pool.rearrange("e k (u p c) o -> k u p e (c o)", u=2, p=P, c=2)
+        nc.sync.dma_start(out=w_nat[0:96, :], in_=weights_pool.rearrange("e k (u f) o -> (e k u) (f o)", u=2))
         src0, dst0 = load_x(0, True)
         for k in range(KC):
-            for u in range(2):
-                nc.sync.dma_start(out=w_raw[:, k, :, 32 * u : 32 * u + 32], in_=wv[k, u])
             nc.sync.dma_start(out=dst0[:, k, :], in_=src0[:, k, :])
         nc.sync.dma_start(
             out=g_bf[:].rearrange("p (b c) -> p b c", b=B),
@@ -179,21 +185,43 @@ def tile_dygcn_pb_t_kernel(tc, x_g, emb, weights_pool, bias_pool, out):
         for b in range(1, NB):
             load_x(b, False)
 
+        def w_planes(g, copy):
+            copy(
+                out=w_prm[:, 4 * g : 4 * g + 4, :].rearrange("p i f -> p f i"),
+                in_=w_nat[:].rearrange("p (f o) -> p f o", o=O)[:, :, 4 * g : 4 * g + 4],
+            )
+
+        def w_turn(g, copy):
+            tpw = ps_t.tile([P, 512], F32, name="tpw", tag="tp")
+            for i in range(4):
+                nc.tensor.transpose(tpw[:, P * i : P * i + P], w_prm[:, 4 * g + i, :].bitcast(F32), perm_f[:])
+            copy(
+                out=w_grp[:]
+                .rearrange("p (k c) -> p k c", k=KC)[:, :, P * g : P * g + P]
+                .rearrange("p k (i c) -> p k i c", i=4),
+                in_=tpw[:].rearrange("p (i k c) -> p k i c", i=4, k=4)[:, 0:KC],
+            )
+
+        w_planes(0, nc.vector.tensor_copy)
+        w_planes(3, nc.scalar.copy)
+        w_planes(1, nc.vector.tensor_copy)
+        w_planes(2, nc.vector.tensor_copy)
+        w_turn(0, nc.scalar.copy)
+        w_turn(3, nc.scalar.copy)
+        w_turn(1, nc.vector.tensor_copy)
+        w_turn(2, nc.vector.tensor_copy)
+        nc.vector.quantize_mx(
+            out=w_cod[:, 0:512].bitcast(FP8X4), scales=w_scl[:, 0:512], in_=w_grp[:, 0:1024].bitcast(BF16)
+        )
+        nc.vector.quantize_mx(
+            out=w_cod[:, 512:768].bitcast(FP8X4), scales=w_scl[:, 512:768], in_=w_grp[:, 1024:1536].bitcast(BF16)
+        )
+
         new_batch(0)
         for k in range(KC):
             transpose_bank(0, 2 * k)
             transpose_bank(0, 2 * k + 1)
-            nc.vector.tensor_copy(
-                out=w_grp[:, k, :].rearrange("p (o e t) -> p o e t", o=O, e=E),
-                in_=w_raw[:, k].rearrange("p e (t o) -> p o e t", t=4),
-            )
-            nc.vector.quantize_mx(
-                out=w_cod[:, 256 * k : 256 * k + 256].bitcast(FP8X4),
-                scales=w_scl[:, 256 * k : 256 * k + 256],
-                in_=w_grp[:, k, :],
-            )
             quantise(0, 512 * k, 512)
-
         bias_product()
 
         for i in range(1, B + 2):

@@ -19,6 +19,7 @@ UNITS = KC * NT
 NB = 6
 BO = NT * O
 GP_LAST = B - 3
+FINE = 3
 
 FLOPS = 2 * B * N * KC * F * E * O + 4 * B * N * E * O
 
@@ -63,9 +64,11 @@ def tile_dygcn_pb_t_kernel(tc, x_g, emb, weights_pool, bias_pool, out):
             xs_of[b] = xs
             src = x_g[b].rearrange("k (p t) f -> p k (t f)", t=NT)
             dst = xs[:].rearrange("p (k c) -> p k c", k=KC)
-            if not split:
+            if split:
+                for k in range(KC):
+                    nc.sync.dma_start(out=dst[:, k, :], in_=src[:, k, :])
+            else:
                 nc.sync.dma_start(out=dst, in_=src)
-            return src, dst
 
         def new_batch(b):
             gr_of[b] = gpool.tile([P, UNITS * 256], F32, name="gr", align_bytes=64)
@@ -131,24 +134,26 @@ def tile_dygcn_pb_t_kernel(tc, x_g, emb, weights_pool, bias_pool, out):
                 op=ADD,
             )
 
-        def finish(b0, nb, terms, width):
+        def finish(b0, nb, terms, width, adder):
             rs = ppool.tile([P, 2 * BO], F32, name="rs")
             nc.vector.tensor_reduce(
                 out=rs[:, 0 : nb * BO], in_=terms.rearrange("p (c e) -> p c e", e=width), axis=AX, op=ADD
             )
             cols = slice(BO * b0, BO * (b0 + nb))
-            nc.vector.tensor_tensor(out=o_sb[:, cols], in0=rs[:, 0 : nb * BO], in1=gb[:, cols], op=ADD)
+            adder.tensor_tensor(out=o_sb[:, cols], in0=rs[:, 0 : nb * BO], in1=gb[:, cols], op=ADD)
             nc.sync.dma_start(
                 out=out[b0 : b0 + nb].rearrange("b (p t) o -> p b (t o)", t=NT),
                 in_=o_sb[:, cols].rearrange("p (b c) -> p b c", b=nb),
             )
 
-        def bias_product():
+        def bias_product_turn():
             tpb = ps_t.tile([P, 1024], BF16, name="tpb", tag="tp")
             for c in range(8):
                 nc.tensor.transpose(tpb[:, P * c : P * c + P], g_bf[:, P * c : P * c + P], ident_b[:])
             nc.scalar.copy(out=g_t[:], in_=tpb[:])
             nc.vector.tensor_copy(out=g_32[:].rearrange("p t e -> p (t e)"), in_=g_bf[:])
+
+        def bias_product_multiply():
             for half in range(2):
                 gp = ps_t.tile([P, 512], F32, name="gp", tag="tp")
                 for c4 in range(4):
@@ -161,6 +166,11 @@ def tile_dygcn_pb_t_kernel(tc, x_g, emb, weights_pool, bias_pool, out):
                         stop=True,
                     )
                 nc.scalar.copy(out=gb[:, 512 * half : 512 * half + 512], in_=gp[:])
+
+        def weigh_and_fold(b, h):
+            weigh(b, h)
+            if b <= GP_LAST:
+                fold_16_to_8(b, h)
 
         make_identity(nc, ident_f[:])
         make_identity(nc, ident_b[:])
@@ -175,15 +185,13 @@ def tile_dygcn_pb_t_kernel(tc, x_g, emb, weights_pool, bias_pool, out):
         nc.vector.tensor_copy(out=perm_f[:, 96:128], in_=ident_f[:, 96:128])
 
         nc.sync.dma_start(out=w_nat[0:96, :], in_=weights_pool.rearrange("e k (u f) o -> (e k u) (f o)", u=2))
-        src0, dst0 = load_x(0, True)
-        for k in range(KC):
-            nc.sync.dma_start(out=dst0[:, k, :], in_=src0[:, k, :])
+        load_x(0, True)
         nc.sync.dma_start(
             out=g_bf[:].rearrange("p (b c) -> p b c", b=B),
             in_=emb.rearrange("b (p t) e -> p b (t e)", t=NT),
         )
         for b in range(1, NB):
-            load_x(b, False)
+            load_x(b, b <= FINE)
 
         def w_planes(g, copy):
             copy(
@@ -222,30 +230,42 @@ def tile_dygcn_pb_t_kernel(tc, x_g, emb, weights_pool, bias_pool, out):
             transpose_bank(0, 2 * k)
             transpose_bank(0, 2 * k + 1)
             quantise(0, 512 * k, 512)
-        bias_product()
+        bias_product_turn()
 
-        for i in range(1, B + 2):
+        for i in range(1, FINE + 1):
+            load_x(i + NB - 1, False)
+            new_batch(i)
+            for j in range(6):
+                transpose_bank(i, j)
+            if i == 1:
+                bias_product_multiply()
+            mx(i - 1, 0)
+            mx(i - 1, 1)
+            quantise(i, 0, 512)
+            quantise(i, 512, 512)
+            weigh_and_fold(i - 1, 0)
+            quantise(i, 1024, 512)
+            weigh_and_fold(i - 1, 1)
+            if i == 3:
+                finish(0, 2, q1_of[0][:], 8, nc.gpsimd)
+
+        for i in range(FINE + 1, B + 2):
             if i < B:
                 if i + NB - 1 < B:
                     load_x(i + NB - 1, False)
                 new_batch(i)
                 for j in range(6):
                     transpose_bank(i, j)
-            if i >= 2:
+            if i >= FINE + 2:
                 mx(i - 2, 0)
                 mx(i - 2, 1)
-            if 2 <= i <= B:
-                quantise(i - 1, 0, 1024)
-                quantise(i - 1, 1024, 512)
-            if i == B + 1:
-                finish(B - 2, 1, pr_of[B - 2][:], E)
-            if i >= 2:
-                weigh(i - 2, 0)
-                if i - 2 <= GP_LAST:
-                    fold_16_to_8(i - 2, 0)
-                weigh(i - 2, 1)
-                if i - 2 <= GP_LAST:
-                    fold_16_to_8(i - 2, 1)
-            if i >= 4 and i % 2 == 0:
-                finish(i - 4, 2, q1_of[(i - 4) // 2][:], 8)
-        finish(B - 1, 1, pr_of[B - 1][:], E)
+                if i <= B:
+                    quantise(i - 1, 0, 1024)
+                    quantise(i - 1, 1024, 512)
+                if i == B + 1:
+                    finish(B - 2, 1, pr_of[B - 2][:], E, nc.gpsimd)
+                weigh_and_fold(i - 2, 0)
+                weigh_and_fold(i - 2, 1)
+                if i % 2 == 0:
+                    finish(i - 4, 2, q1_of[(i - 4) // 2][:], 8, nc.gpsimd)
+        finish(B - 1, 1, pr_of[B - 1][:], E, nc.vector)

@@ -146,6 +146,28 @@ def tile_dygcn_pb_t_kernel(tc, x_g, emb, weights_pool, bias_pool, out):
                 in_=o_sb[:, cols].rearrange("p (b c) -> p b c", b=nb),
             )
 
+        def finish_on_gpsimd(b0):
+            terms = q1_of[b0 // 2][:]
+            width = 8
+            while width > 1:
+                half = width // 2
+                tv = terms.rearrange("p (c e) -> p c e", e=width)
+                nxt = ppool.tile([P, 2 * BO * half], F32, name="fold%d" % half)
+                nc.gpsimd.tensor_tensor(
+                    out=nxt[:].rearrange("p (c e) -> p c e", e=half),
+                    in0=tv[:, :, 0:half],
+                    in1=tv[:, :, half:width],
+                    op=ADD,
+                )
+                terms = nxt[:]
+                width = half
+            cols = slice(BO * b0, BO * (b0 + 2))
+            nc.gpsimd.tensor_tensor(out=o_sb[:, cols], in0=terms, in1=gb[:, cols], op=ADD)
+            nc.sync.dma_start(
+                out=out[b0 : b0 + 2].rearrange("b (p t) o -> p b (t o)", t=NT),
+                in_=o_sb[:, cols].rearrange("p (b c) -> p b c", b=2),
+            )
+
         def bias_product_turn():
             tpb = ps_t.tile([P, 1024], BF16, name="tpb", tag="tp")
             for c in range(8):
@@ -266,6 +288,8 @@ def tile_dygcn_pb_t_kernel(tc, x_g, emb, weights_pool, bias_pool, out):
                     finish(B - 2, 1, pr_of[B - 2][:], E, nc.gpsimd)
                 weigh_and_fold(i - 2, 0)
                 weigh_and_fold(i - 2, 1)
-                if i % 2 == 0:
+                if i == B:
+                    finish_on_gpsimd(i - 4)
+                elif i % 2 == 0:
                     finish(i - 4, 2, q1_of[(i - 4) // 2][:], 8, nc.gpsimd)
         finish(B - 1, 1, pr_of[B - 1][:], E, nc.vector)

from contextlib import ExitStack

import concourse.mybir as mybir
from concourse.masks import make_identity

BF16 = mybir.dt.bfloat16
F32 = mybir.dt.float32
U32 = mybir.dt.uint32
U8 = mybir.dt.uint8
FP8X4 = mybir.dt.float8_e4m3fn_x4
ADD = mybir.AluOpType.add
MULT = mybir.AluOpType.mult
AX = mybir.AxisListType.X

P = 128
B, KC, N, F, O, E = 16, 3, 512, 512, 16, 16
NT = N // P
UNITS = KC * NT
NB = 6
BO = NT * O
GP_LAST = B - 3
FINE = 3

FLOPS = 2 * B * N * KC * F * E * O + 4 * B * N * E * O


def tile_dygcn_pb_t_kernel(tc, x_g, emb, weights_pool, bias_pool, out):
    nc = tc.nc
    with ExitStack() as ctx:
        const = ctx.enter_context(tc.tile_pool(name="const", bufs=1))
        xpool = ctx.enter_context(tc.tile_pool(name="xpool", bufs=NB))
        gpool = ctx.enter_context(tc.tile_pool(name="gpool", bufs=3))
        cpool = ctx.enter_context(tc.tile_pool(name="cpool", bufs=3))
        ppool = ctx.enter_context(tc.tile_pool(name="ppool", bufs=4))
        ps_t = ctx.enter_context(tc.psum_pool(name="ps_t", bufs=6))
        ps_z = ctx.enter_context(tc.psum_pool(name="ps_z", bufs=2))
        ctx.enter_context(tc.manual_schedule())

        ident_f = const.tile([P, P], F32, name="ident_f")
        ident_b = const.tile([P, P], BF16, name="ident_b")
        perm_f = const.tile([P, P], F32, name="perm_f")
        w_nat = const.tile([P, 256 * O], BF16, name="w_nat")
        w_prm = const.tile([P, O, 256], BF16, name="w_prm")
        w_grp = const.tile([P, KC * 512], F32, name="w_grp", align_bytes=64)
        w_cod = const.tile([P, KC * 256], U32, name="w_cod", align_bytes=64)
        w_scl = const.tile([P, KC * 256], U8, name="w_scl", align_bytes=64)
        g_bf = const.tile([P, B * NT * E], BF16, name="g_bf")
        g_32 = const.tile([P, B * NT, E], F32, name="g_32")
        g_t = const.tile([P, B * NT * E], BF16, name="g_t")
        bdiag = const.tile([P, P], BF16, name="bdiag")
        gb = const.tile([P, B * BO], F32, name="gb")
        o_sb = const.tile([P, B * BO], F32, name="o_sb")

        xs_of = {}
        gr_of = {}
        cd_of = {}
        sc_of = {}
        zp_of = {}
        pr_of = {}
        q1_of = {}

        def load_x(b, split):
            xs = xpool.tile([P, KC * NT * F], BF16, name="xs")
            xs_of[b] = xs
            src = x_g[b].rearrange("k (p t) f -> p k (t f)", t=NT)
            dst = xs[:].rearrange("p (k c) -> p k c", k=KC)
            if split:
                for k in range(KC):
                    nc.sync.dma_start(out=dst[:, k, :], in_=src[:, k, :])
            else:
                nc.sync.dma_start(out=dst, in_=src)

        def new_batch(b):
            gr_of[b] = gpool.tile([P, UNITS * 256], F32, name="gr", align_bytes=64)
            cd_of[b] = cpool.tile([P, UNITS * P], U32, name="cd", align_bytes=64)
            sc_of[b] = cpool.tile([P, UNITS * P], U8, name="sc", align_bytes=64)

        def transpose_bank(b, j):
            xw = xs_of[b][:].bitcast(F32)
            tp = ps_t.tile([P, 512], F32, name="tp", tag="tp")
            for s in range(4):
                c0 = P * (4 * j + s)
                nc.tensor.transpose(tp[:, P * s : P * s + P], xw[:, c0 : c0 + P], ident_f[:])
            nc.scalar.copy(
                out=gr_of[b][:, 512 * j : 512 * j + 512].rearrange("p (a n u) -> p a n u", a=2, u=2),
                in_=tp[:].rearrange("p (a u n) -> p a n u", a=2, u=2),
            )

        def quantise(b, c0, cw):
            nc.vector.quantize_mx(
                out=cd_of[b][:, c0 : c0 + cw].bitcast(FP8X4),
                scales=sc_of[b][:, c0 : c0 + cw],
                in_=gr_of[b][:, 2 * c0 : 2 * (c0 + cw)].bitcast(BF16),
            )

        def mx(b, h):
            cd = cd_of[b]
            sc = sc_of[b]
            zp = ps_z.tile([P, 512], F32, name="zp", tag="zp")
            zp_of[(b, h)] = zp
            for a in range(2):
                for k in range(KC):
                    c0 = P * (NT * k + 2 * h + a)
                    nc.tensor.matmul_mx(
                        out=zp[:, 256 * a : 256 * a + 256],
                        lhsT=cd[:, c0 : c0 + P].bitcast(FP8X4),
                        lhsT_scale=sc[:, c0 : c0 + P],
                        rhs=w_cod[:, 256 * k : 256 * k + 256].bitcast(FP8X4),
                        rhs_scale=w_scl[:, 256 * k : 256 * k + 256],
                        start=(k == 0),
                        stop=(k == KC - 1),
                    )

        def weigh(b, h):
            if h == 0:
                pr_of[b] = ppool.tile([P, NT * O * E], F32, name="pr")
            t0 = NT * b + 2 * h
            nc.vector.tensor_tensor(
                out=pr_of[b][:, 512 * h : 512 * h + 512].rearrange("p (a o e) -> p a o e", a=2, o=O),
                in0=zp_of[(b, h)][:].rearrange("p (a o e) -> p a o e", a=2, o=O),
                in1=g_32[:, t0 : t0 + 2, :].unsqueeze(2).to_broadcast([P, 2, O, E]),
                op=MULT,
            )

        def fold_16_to_8(b, h):
            if h == 0 and b % 2 == 0:
                q1_of[b // 2] = ppool.tile([P, 2 * BO * 8], F32, name="q1")
            pv = pr_of[b][:, 512 * h : 512 * h + 512].rearrange("p (c e) -> p c e", e=E)
            c0 = 512 * (b % 2) + 256 * h
            nc.gpsimd.tensor_tensor(
                out=q1_of[b // 2][:, c0 : c0 + 256].rearrange("p (c e) -> p c e", e=8),
                in0=pv[:, :, 0:8],
                in1=pv[:, :, 8:16],
                op=ADD,
            )

        def finish(b0, nb, terms, width, adder):
            rs = ppool.tile([P, 2 * BO], F32, name="rs")
            nc.vector.tensor_reduce(
                out=rs[:, 0 : nb * BO], in_=terms.rearrange("p (c e) -> p c e", e=width), axis=AX, op=ADD
            )
            cols = slice(BO * b0, BO * (b0 + nb))
            adder.tensor_tensor(out=o_sb[:, cols], in0=rs[:, 0 : nb * BO], in1=gb[:, cols], op=ADD)
            nc.sync.dma_start(
                out=out[b0 : b0 + nb].rearrange("b (p t) o -> p b (t o)", t=NT),
                in_=o_sb[:, cols].rearrange("p (b c) -> p b c", b=nb),
            )

        def finish_on_gpsimd(b0):
            terms = q1_of[b0 // 2][:]
            width = 8
            while width > 1:
                half = width // 2
                tv = terms.rearrange("p (c e) -> p c e", e=width)
                nxt = ppool.tile([P, 2 * BO * half], F32, name="fold%d" % half)
                nc.gpsimd.tensor_tensor(
                    out=nxt[:].rearrange("p (c e) -> p c e", e=half),
                    in0=tv[:, :, 0:half],
                    in1=tv[:, :, half:width],
                    op=ADD,
                )
                terms = nxt[:]
                width = half
            cols = slice(BO * b0, BO * (b0 + 2))
            nc.gpsimd.tensor_tensor(out=o_sb[:, cols], in0=terms, in1=gb[:, cols], op=ADD)
            nc.sync.dma_start(
                out=out[b0 : b0 + 2].rearrange("b (p t) o -> p b (t o)", t=NT),
                in_=o_sb[:, cols].rearrange("p (b c) -> p b c", b=2),
            )

        def bias_product_turn():
            tpb = ps_t.tile([P, 1024], BF16, name="tpb", tag="tp")
            for c in range(8):
                nc.tensor.transpose(tpb[:, P * c : P * c + P], g_bf[:, P * c : P * c + P], ident_b[:])
            nc.scalar.copy(out=g_t[:], in_=tpb[:])
            nc.vector.tensor_copy(out=g_32[:].rearrange("p t e -> p (t e)"), in_=g_bf[:])

        def bias_product_multiply():
            for half in range(2):
                gp = ps_t.tile([P, 512], F32, name="gp", tag="tp")
                for c4 in range(4):
                    c = 4 * half + c4
                    nc.tensor.matmul(
                        gp[:, P * c4 : P * c4 + P],
                        lhsT=g_t[:, P * c : P * c + P],
                        rhs=bdiag[:],
                        start=True,
                        stop=True,
                    )
                nc.scalar.copy(out=gb[:, 512 * half : 512 * half + 512], in_=gp[:])

        def weigh_and_fold(b, h):
            weigh(b, h)
            if b <= GP_LAST:
                fold_16_to_8(b, h)

        make_identity(nc, ident_f[:])
        make_identity(nc, ident_b[:])
        nc.vector.memset(bdiag[:], 0.0)
        nc.vector.memset(w_nat[96:128, :], 0.0)
        for i in range(8):
            nc.gpsimd.dma_start(out=bdiag[16 * i : 16 * i + 16, 16 * i : 16 * i + 16], in_=bias_pool)
        nc.vector.tensor_copy(
            out=perm_f[:, 0:96].rearrange("p (k e u) -> p k e u", k=KC, e=E),
            in_=ident_f[:, 0:96].rearrange("p (e k u) -> p k e u", e=E, k=KC),
        )
        nc.vector.tensor_copy(out=perm_f[:, 96:128], in_=ident_f[:, 96:128])

        nc.sync.dma_start(out=w_nat[0:96, :], in_=weights_pool.rearrange("e k (u f) o -> (e k u) (f o)", u=2))
        load_x(0, True)
        nc.sync.dma_start(
            out=g_bf[:].rearrange("p (b c) -> p b c", b=B),
            in_=emb.rearrange("b (p t) e -> p b (t e)", t=NT),
        )
        for b in range(1, NB):
            load_x(b, b <= FINE)

        def w_planes(g, copy):
            copy(
                out=w_prm[:, 4 * g : 4 * g + 4, :].rearrange("p i f -> p f i"),
                in_=w_nat[:].rearrange("p (f o) -> p f o", o=O)[:, :, 4 * g : 4 * g + 4],
            )

        def w_turn(g, copy):
            tpw = ps_t.tile([P, 512], F32, name="tpw", tag="tp")
            for i in range(4):
                nc.tensor.transpose(tpw[:, P * i : P * i + P], w_prm[:, 4 * g + i, :].bitcast(F32), perm_f[:])
            copy(
                out=w_grp[:]
                .rearrange("p (k c) -> p k c", k=KC)[:, :, P * g : P * g + P]
                .rearrange("p k (i c) -> p k i c", i=4),
                in_=tpw[:].rearrange("p (i k c) -> p k i c", i=4, k=4)[:, 0:KC],
            )

        w_planes(0, nc.vector.tensor_copy)
        w_planes(3, nc.scalar.copy)
        w_planes(1, nc.vector.tensor_copy)
        w_planes(2, nc.vector.tensor_copy)
        w_turn(0, nc.scalar.copy)
        w_turn(3, nc.scalar.copy)
        w_turn(1, nc.vector.tensor_copy)
        w_turn(2, nc.vector.tensor_copy)
        nc.vector.quantize_mx(
            out=w_cod[:, 0:512].bitcast(FP8X4), scales=w_scl[:, 0:512], in_=w_grp[:, 0:1024].bitcast(BF16)
        )
        nc.vector.quantize_mx(
            out=w_cod[:, 512:768].bitcast(FP8X4), scales=w_scl[:, 512:768], in_=w_grp[:, 1024:1536].bitcast(BF16)
        )

        new_batch(0)
        for k in range(KC):
            transpose_bank(0, 2 * k)
            transpose_bank(0, 2 * k + 1)
            quantise(0, 512 * k, 512)
        bias_product_turn()

        for i in range(1, FINE + 1):
            load_x(i + NB - 1, False)
            new_batch(i)
            for j in range(6):
                transpose_bank(i, j)
            if i == 1:
                bias_product_multiply()
            mx(i - 1, 0)
            mx(i - 1, 1)
            quantise(i, 0, 512)
            quantise(i, 512, 512)
            weigh_and_fold(i - 1, 0)
            quantise(i, 1024, 512)
            weigh_and_fold(i - 1, 1)
            if i == 3:
                finish(0, 2, q1_of[0][:], 8, nc.gpsimd)

        for i in range(FINE + 1, B + 2):
            if i < B:
                if i + NB - 1 < B:
                    load_x(i + NB - 1, False)
                new_batch(i)
                for j in range(6):
                    transpose_bank(i, j)
            if i >= FINE + 2:
                mx(i - 2, 0)
                mx(i - 2, 1)
                if i <= B:
                    quantise(i - 1, 0, 1024)
                    quantise(i - 1, 1024, 512)
                if i == B + 1:
                    finish(B - 2, 1, pr_of[B - 2][:], E, nc.gpsimd)
                weigh_and_fold(i - 2, 0)
                weigh_and_fold(i - 2, 1)
                if i == B:
                    finish_on_gpsimd(i - 4)
                elif i % 2 == 0:
                    finish(i - 4, 2, q1_of[(i - 4) // 2][:], 8, nc.gpsimd)
        finish(B - 1, 1, pr_of[B - 1][:], E, nc.vector)
